import numpy as np
import ml_dtypes


def mxq(x, axis, fmt="e4m3"):
    dtype, down = {"e4m3": (ml_dtypes.float8_e4m3fn, 7), "e5m2": (ml_dtypes.float8_e5m2, 14)}[fmt]
    v = np.moveaxis(np.asarray(x, np.float32).astype(ml_dtypes.bfloat16).astype(np.float64), axis, -1)
    blocks = v.reshape(v.shape[:-1] + (-1, 32))
    amax = np.abs(blocks).max(-1, keepdims=True)
    byte = np.maximum(np.where(amax > 0, np.frexp(amax)[1] - 1 + 127, 0) - down, 1)
    scale = np.exp2(byte - 127.0)
    codes = (blocks / scale).astype(np.float32).astype(dtype).astype(np.float64)
    return np.moveaxis((codes * scale).reshape(v.shape), -1, axis)


WIDE = False


def mx_kscale(k):
    if not WIDE:
        return np.ones(k)
    levels = np.array([10, -10, 5, -5, 0])
    a = np.random.permutation(np.resize(levels, k // 512 * 4)).reshape(k // 512, 4)
    idx = np.arange(k)
    return np.exp2(a[idx // 512, idx % 128 // 32])


BF16 = ml_dtypes.bfloat16


def bf(x):
    return np.asarray(x, np.float32).astype(BF16)


def f64(x):
    return np.asarray(x).astype(np.float64)


C, G, P, E = 512, 2048, 16, 192


def setup_inputs():
    s = mx_kscale(G)
    return {"x": bf(np.random.standard_normal((C, G)) * s),
            "mask": bf(np.random.randint(0, 2, (G, P))),
            "W": bf(np.random.standard_normal((G, P * E)) * 1.4 / np.sqrt(G) / s[:, None]),
            "b": bf(np.random.standard_normal(P * E) * 0.3)}


def reference(x, mask, W, b):
    mask_rep = np.repeat(f64(mask), E, axis=1)
    out = (mxq(f64(x), 1, "e4m3") @ mxq(f64(W) * mask_rep, 0, "e4m3")) + f64(b)
    out = out.reshape(C, E, P).transpose(0, 2, 1)
    return out

@@ -1,0 +1,286 @@
+from contextlib import ExitStack
+
+import concourse.mybir as mybir
+from concourse.masks import make_identity
+
+FLOPS = 2 * 512 * 2048 * 3072
+
+BF16 = mybir.dt.bfloat16
+F32 = mybir.dt.float32
+U32 = mybir.dt.uint32
+U8 = mybir.dt.uint8
+FP8X4 = mybir.dt.float8_e4m3fn_x4
+
+P = 128
+PASSES = 4
+QW = 192
+MANUAL = False
+
+LOAD_ORDER = ((0, 0), (0, 1), "x0", "x1", (0, 2), (0, 3), (1, 0), (1, 1), "bias", (1, 2), (1, 3), (2, 0), (2, 1), (2, 2), (2, 3))
+SUBS = {(0, 0): ((0, 384), (384, 1024))}
+V_UNITS = (5, 18, 23, 28)
+HEAD_MASKS = 24
+X_MASKS = 3
+A_MASKS = 16
+B_MASKS = 0
+A_EXITS = 2
+B_EXITS = 2
+GRP_BUFS = 5
+CODE_BUFS = 8
+XG_BUFS = 3
+
+
+def tile_featureembed_kernel(tc, x, mask, W, b, out):
+    nc = tc.nc
+    mult = mybir.AluOpType.mult
+    add = mybir.AluOpType.add
+    with ExitStack() as ctx:
+        if MANUAL:
+            ctx.enter_context(tc.manual_schedule())
+        const = ctx.enter_context(tc.tile_pool(name="const", bufs=1))
+        rawp = ctx.enter_context(tc.tile_pool(name="raw", bufs=1))
+        grpp = ctx.enter_context(tc.tile_pool(name="grp", bufs=GRP_BUFS))
+        xgp = ctx.enter_context(tc.tile_pool(name="xg", bufs=XG_BUFS))
+        codep = ctx.enter_context(tc.tile_pool(name="code", bufs=CODE_BUFS))
+        outp = ctx.enter_context(tc.tile_pool(name="outp", bufs=1))
+        psum = ctx.enter_context(tc.psum_pool(name="psum", bufs=8))
+
+        mask_sb = const.tile([P, PASSES, 64], BF16, name="mask_sb")
+        nc.sync.dma_start(
+            out=mask_sb[:], in_=mask.rearrange("(g p t) q -> p g (t q)", g=PASSES, p=P, t=4)
+        )
+        w_view = W.rearrange("(g p t) j -> g p t j", g=PASSES, p=P, t=4)
+        x_view = x.rearrange("(a c p) g -> a p c g", a=2, c=2, p=P)
+        bias_sb = const.tile([P, 3072], BF16, name="bias_sb")
+        raw = {}
+        x_sb = {}
+        seg_cols = {}
+        mask_queue = []
+        for item in LOAD_ORDER:
+            if item == "x0" or item == "x1":
+                pr = 0 if item == "x0" else 1
+                x_sb[pr] = const.tile([P, 2, 2048], BF16, name="x_sb%d" % pr)
+                nc.sync.dma_start(out=x_sb[pr][:], in_=x_view[pr])
+            elif item == "bias":
+                nc.sync.dma_start(out=bias_sb[:], in_=b.partition_broadcast(P))
+            else:
+                s, gp = item
+                seg_cols[item] = SUBS.get(item, ((1024 * s, 1024 * s + 1024),))
+                for si in range(len(seg_cols[item])):
+                    c0, c1 = seg_cols[item][si]
+                    tl = rawp.tile([P, 4, c1 - c0], BF16, name="raw%d_%d_%d" % (s, gp, si))
+                    nc.sync.dma_start(out=tl[:], in_=w_view[gp][:, :, c0:c1])
+                    raw[(s, gp, si)] = tl
+                    for q in range(c0 // QW, (c1 - 1) // QW + 1):
+                        for t in range(4):
+                            mask_queue.append((s, gp, si, q, t))
+
+        ident = const.tile([P, P], F32, name="ident")
+        make_identity(nc, ident[:])
+        maskf = const.tile([P, PASSES * 64], F32, name="maskf")
+        nc.vector.tensor_copy(out=maskf[:], in_=mask_sb[:].rearrange("p g c -> p (g c)"))
+        bias_v8 = bias_sb[:].rearrange("p (e o i) -> p o i e", o=2, i=8)
+        bias_v4 = bias_sb[:].rearrange("p (e q i) -> p q i e", q=4, i=4)
+        xq = const.tile([P, PASSES, 512], U32, name="xq", align_bytes=64)
+        xs = const.tile([P, PASSES, 512], U8, name="xs", align_bytes=64)
+
+        units = []
+        for s in range(2):
+            for gp in range(PASSES):
+                for o in range(2):
+                    units.append((s, gp, o))
+        for bq in range(4):
+            for gp in range(PASSES):
+                units.append((2, gp, bq))
+
+        st = {"mi": 0, "xdone": False, "q": 0, "mm": 0, "ex": 0, "open": 0}
+        pend_q = []
+        pend_mm = []
+        exit_q = []
+        grp_of = {}
+        codes = {}
+        acc = {}
+        o_sb = {}
+
+        def emit_masks(k):
+            for n in range(k):
+                if st["mi"] < len(mask_queue):
+                    s, gp, si, q, t = mask_queue[st["mi"]]
+                    st["mi"] += 1
+                    c0, c1 = seg_cols[(s, gp)][si]
+                    a = max(c0, q * QW) - c0
+                    z = min(c1, q * QW + QW) - c0
+                    tl = raw[(s, gp, si)]
+                    idx = gp * 64 + t * 16 + q
+                    nc.vector.tensor_scalar(
+                        out=tl[:, t, a:z],
+                        in0=tl[:, t, a:z],
+                        scalar1=maskf[:, idx : idx + 1],
+                        scalar2=None,
+                        op0=mult,
+                    )
+
+        def emit_masks_through(s, gp, si):
+            want = 0
+            for n in range(len(mask_queue)):
+                if mask_queue[n][0:3] == (s, gp, si):
+                    want = n + 1
+            emit_masks(max(0, want - st["mi"]))
+
+        def regroup(j, subs=None):
+            s, gp, c = units[j]
+            width = 8 if s < 2 else 4
+            ncol = 64 * width
+            if j not in grp_of:
+                grp_of[j] = grpp.tile([P, ncol, 4], BF16, name="grp", tag="grp", align_bytes=64)
+            dst_v = grp_of[j][:].rearrange("p (e i) t -> p e t i", i=width)
+            for si in range(len(seg_cols[(s, gp)])):
+                if subs is None or si in subs:
+                    emit_masks_through(s, gp, si)
+                    c0, c1 = seg_cols[(s, gp)][si]
+                    src = raw[(s, gp, si)][:].rearrange(
+                        "p t (e o i) -> p o e t i", o=16 // width, i=width
+                    )[:, c]
+                    dst = dst_v[:, c0 // 16 - 64 * s : c1 // 16 - 64 * s]
+                    if j in V_UNITS:
+                        nc.vector.tensor_copy(out=dst, in_=src)
+                    else:
+                        nc.scalar.copy(out=dst, in_=src)
+
+        def quantise(j):
+            s, gp, c = units[j]
+            ncol = 512 if s < 2 else 256
+            wq = codep.tile([P, ncol], U32, name="wq", tag="wq", align_bytes=64)
+            ws = codep.tile([P, ncol], U8, name="ws", tag="ws", align_bytes=64)
+            nc.vector.quantize_mx(
+                out=wq[:].bitcast(FP8X4),
+                scales=ws[:],
+                in_=grp_of[j][:].rearrange("p c t -> p (c t)"),
+            )
+            codes[j] = (wq, ws)
+
+        def flush_q():
+            while st["q"] < len(pend_q):
+                j = pend_q[st["q"]]
+                st["q"] += 1
+                quantise(j)
+                pend_mm.append(j)
+
+        def matmuls(j):
+            s, gp, c = units[j]
+            ncol = 512 if s < 2 else 256
+            wq, ws = codes[j]
+            for ct in range(4):
+                key = (s, c, ct)
+                if gp == 0:
+                    acc[key] = psum.tile([P, ncol], F32, name="acc", tag="bank")
+                    st["open"] += 1
+                cs = slice(ct * P, (ct + 1) * P)
+                nc.tensor.matmul_mx(
+                    out=acc[key][:],
+                    lhsT=xq[:, gp, cs].bitcast(FP8X4),
+                    lhsT_scale=xs[:, gp, cs],
+                    rhs=wq[:].bitcast(FP8X4),
+                    rhs_scale=ws[:],
+                    start=(gp == 0),
+                    stop=(gp == PASSES - 1),
+                )
+                if gp == PASSES - 1:
+                    exit_q.append(key)
+
+        def flush_mm():
+            while st["xdone"] and st["mm"] < len(pend_mm):
+                j = pend_mm[st["mm"]]
+                if units[j][1] == 0 and st["open"] + 4 > 8:
+                    return
+                st["mm"] += 1
+                matmuls(j)
+
+        def emit_exit():
+            if st["ex"] >= len(exit_q):
+                return
+            key = exit_q[st["ex"]]
+            st["ex"] += 1
+            st["open"] -= 1
+            s, c, ct = key
+            if s < 2:
+                if s == 0:
+                    o_sb[(c, ct)] = outp.tile([P, 8, 192], F32, name="o%d_%d" % (c, ct))
+                nc.vector.tensor_tensor(
+                    out=o_sb[(c, ct)][:, :, 64 * s : 64 * s + 64],
+                    in0=acc[key][:].rearrange("p (e i) -> p i e", i=8),
+                    in1=bias_v8[:, c, :, 64 * s : 64 * s + 64],
+                    op=add,
+                )
+            else:
+                rows = slice(4 * (c % 2), 4 * (c % 2) + 4)
+                ot = o_sb[(c // 2, ct)]
+                nc.vector.tensor_tensor(
+                    out=ot[:, rows, 128:192],
+                    in0=acc[key][:].rearrange("p (e i) -> p i e", i=4),
+                    in1=bias_v4[:, c, :, 128:192],
+                    op=add,
+                )
+                nc.sync.dma_start(
+                    out=out[ct * P : (ct + 1) * P, 4 * c : 4 * c + 4, :], in_=ot[:, rows, :]
+                )
+
+        def x_block():
+            flush_q()
+            prev = []
+            for k in range(8):
+                pr, gp = k // 4, k % 4
+                xw = x_sb[pr][:].bitcast(F32).rearrange("p c (g w u) -> p c g u w", g=PASSES, u=2)
+                xt = psum.tile([P, 2, 256], F32, name="xt", tag="bank")
+                for u in range(2):
+                    for cl in range(2):
+                        nc.tensor.transpose(
+                            xt[:, u, cl * P : (cl + 1) * P], xw[:, cl, gp, u, :], ident[:]
+                        )
+                xg = xgp.tile([P, 256, 4], BF16, name="xg", align_bytes=64)
+                nc.scalar.copy(out=xg[:].bitcast(F32), in_=xt[:].rearrange("p u c -> p c u"))
+                prev.append((xg, pr, gp))
+                if k > 0:
+                    x_quant(prev[k - 1])
+                emit_masks(X_MASKS)
+            x_quant(prev[7])
+            st["xdone"] = True
+            flush_mm()
+
+        def x_quant(item):
+            xg, pr, gp = item
+            cs = slice(pr * 256, (pr + 1) * 256)
+            nc.vector.quantize_mx(
+                out=xq[:, gp, cs].bitcast(FP8X4),
+                scales=xs[:, gp, cs],
+                in_=xg[:].rearrange("p c t -> p (c t)"),
+            )
+
+        for si in range(len(seg_cols[(0, 0)])):
+            regroup(0, (si,))
+            regroup(1, (si,))
+            if si == 0:
+                emit_masks_through(0, 0, 1)
+        emit_masks(HEAD_MASKS)
+        pend_q.append(0)
+        pend_q.append(1)
+        for j in (2, 3, "X") + tuple(range(4, 32)):
+            if j == "X":
+                x_block()
+            else:
+                regroup(j)
+                if j in V_UNITS:
+                    pend_q.append(j)
+                else:
+                    flush_q()
+                    pend_q.append(j)
+                    part_a = units[j][0] < 2
+                    emit_masks(A_MASKS if part_a else B_MASKS)
+                    flush_mm()
+                    for n in range(A_EXITS if part_a else B_EXITS):
+                        emit_exit()
+                    flush_mm()
+        flush_q()
+        for n in range(64):
+            flush_mm()
+            emit_exit()

@@ -7,6 +7,7 @@ FLOPS = 2 * 512 * 2048 * 3072
 
 BF16 = mybir.dt.bfloat16
 F32 = mybir.dt.float32
+I32 = mybir.dt.int32
 U32 = mybir.dt.uint32
 U8 = mybir.dt.uint8
 FP8X4 = mybir.dt.float8_e4m3fn_x4
@@ -15,19 +16,21 @@ P = 128
 PASSES = 4
 QW = 192
 MANUAL = False
+AND_MASK = True
 
-LOAD_ORDER = ((0, 0), (0, 1), "x0", "x1", (0, 2), (0, 3), (1, 0), (1, 1), "bias", (1, 2), (1, 3), (2, 0), (2, 1), (2, 2), (2, 3))
+LOAD_ORDER = ((0, 0), (0, 1), "x0", "x1", (0, 2), (0, 3), (1, 0), "bias", (1, 1), (1, 2), (1, 3), (2, 0), (2, 1), (2, 2), (2, 3))
 SUBS = {(0, 0): ((0, 384), (384, 1024))}
-V_UNITS = (5, 18, 23, 28)
-HEAD_MASKS = 24
-X_MASKS = 3
-A_MASKS = 16
+V_UNITS = ()
+HEAD_MASKS = 2
+X_MASKS = 0
+A_MASKS = 1
 B_MASKS = 0
 A_EXITS = 2
 B_EXITS = 2
 GRP_BUFS = 5
 CODE_BUFS = 8
 XG_BUFS = 3
+BIAS_SLOT = 6
 
 
 def tile_featureembed_kernel(tc, x, mask, W, b, out):
@@ -45,13 +48,15 @@ def tile_featureembed_kernel(tc, x, mask, W, b, out):
         outp = ctx.enter_context(tc.tile_pool(name="outp", bufs=1))
         psum = ctx.enter_context(tc.psum_pool(name="psum", bufs=8))
 
-        mask_sb = const.tile([P, PASSES, 64], BF16, name="mask_sb")
+        mask_sb = const.tile([P, PASSES * 64], BF16, name="mask_sb")
         nc.sync.dma_start(
-            out=mask_sb[:], in_=mask.rearrange("(g p t) q -> p g (t q)", g=PASSES, p=P, t=4)
+            out=mask_sb[:].rearrange("p (g c) -> p g c", g=PASSES),
+            in_=mask.rearrange("(g p t) q -> p g (t q)", g=PASSES, p=P, t=4),
         )
         w_view = W.rearrange("(g p t) j -> g p t j", g=PASSES, p=P, t=4)
         x_view = x.rearrange("(a c p) g -> a p c g", a=2, c=2, p=P)
         bias_sb = const.tile([P, 3072], BF16, name="bias_sb")
+        bias_pe = const.tile([P, 16, 192], BF16, name="bias_pe")
         raw = {}
         x_sb = {}
         seg_cols = {}
@@ -71,16 +76,29 @@ def tile_featureembed_kernel(tc, x, mask, W, b, out):
                     tl = rawp.tile([P, 4, c1 - c0], BF16, name="raw%d_%d_%d" % (s, gp, si))
                     nc.sync.dma_start(out=tl[:], in_=w_view[gp][:, :, c0:c1])
                     raw[(s, gp, si)] = tl
-                    for q in range(c0 // QW, (c1 - 1) // QW + 1):
-                        for t in range(4):
-                            mask_queue.append((s, gp, si, q, t))
+                    if AND_MASK:
+                        qa = (c0 + QW - 1) // QW
+                        qz = c1 // QW
+                        if c0 < qa * QW:
+                            mask_queue.append((s, gp, si, qa - 1, qa, c0, qa * QW))
+                        mask_queue.append((s, gp, si, qa, qz, qa * QW, qz * QW))
+                        if qz * QW < c1:
+                            mask_queue.append((s, gp, si, qz, qz + 1, qz * QW, c1))
+                    else:
+                        for q in range(c0 // QW, (c1 - 1) // QW + 1):
+                            for t in range(4):
+                                mask_queue.append((s, gp, si, q, t))
 
         ident = const.tile([P, P], F32, name="ident")
         make_identity(nc, ident[:])
-        maskf = const.tile([P, PASSES * 64], F32, name="maskf")
-        nc.vector.tensor_copy(out=maskf[:], in_=mask_sb[:].rearrange("p g c -> p (g c)"))
-        bias_v8 = bias_sb[:].rearrange("p (e o i) -> p o i e", o=2, i=8)
-        bias_v4 = bias_sb[:].rearrange("p (e q i) -> p q i e", q=4, i=4)
+        if AND_MASK:
+            mtab = const.tile([P, PASSES * 64], I32, name="mtab")
+            nc.vector.tensor_scalar(
+                out=mtab[:], in0=mask_sb[:], scalar1=-1.0, scalar2=None, op0=mult
+            )
+        else:
+            mtab = const.tile([P, PASSES * 64], F32, name="mtab")
+            nc.vector.tensor_copy(out=mtab[:], in_=mask_sb[:])
         xq = const.tile([P, PASSES, 512], U32, name="xq", align_bytes=64)
         xs = const.tile([P, PASSES, 512], U8, name="xs", align_bytes=64)
 
@@ -93,7 +111,7 @@ def tile_featureembed_kernel(tc, x, mask, W, b, out):
             for gp in range(PASSES):
                 units.append((2, gp, bq))
 
-        st = {"mi": 0, "xdone": False, "q": 0, "mm": 0, "ex": 0, "open": 0}
+        st = {"mi": 0, "xdone": False, "q": 0, "mm": 0, "ex": 0, "open": 0, "slot": 0}
         pend_q = []
         pend_mm = []
         exit_q = []
@@ -105,20 +123,37 @@ def tile_featureembed_kernel(tc, x, mask, W, b, out):
         def emit_masks(k):
             for n in range(k):
                 if st["mi"] < len(mask_queue):
-                    s, gp, si, q, t = mask_queue[st["mi"]]
+                    item = mask_queue[st["mi"]]
                     st["mi"] += 1
+                    s, gp, si = item[0:3]
                     c0, c1 = seg_cols[(s, gp)][si]
-                    a = max(c0, q * QW) - c0
-                    z = min(c1, q * QW + QW) - c0
                     tl = raw[(s, gp, si)]
-                    idx = gp * 64 + t * 16 + q
-                    nc.vector.tensor_scalar(
-                        out=tl[:, t, a:z],
-                        in0=tl[:, t, a:z],
-                        scalar1=maskf[:, idx : idx + 1],
-                        scalar2=None,
-                        op0=mult,
-                    )
+                    if AND_MASK:
+                        q0, q1, a, z = item[3:7]
+                        words = tl[:].bitcast(I32)[:, :, (a - c0) // 2 : (z - c0) // 2]
+                        tab = mtab[:, gp * 64 : gp * 64 + 64].rearrange("p (t q) -> p t q", t=4)
+                        if q1 - q0 > 1:
+                            words = words.rearrange("p t (q w) -> p t q w", q=q1 - q0)
+                            sel = tab[:, :, q0:q1].unsqueeze(3).to_broadcast(
+                                [P, 4, q1 - q0, QW // 2]
+                            )
+                        else:
+                            sel = tab[:, :, q0:q1].to_broadcast([P, 4, (z - a) // 2])
+                        nc.vector.tensor_tensor(
+                            out=words, in0=words, in1=sel, op=mybir.AluOpType.bitwise_and
+                        )
+                    else:
+                        q, t = item[3:5]
+                        a = max(c0, q * QW) - c0
+                        z = min(c1, q * QW + QW) - c0
+                        idx = gp * 64 + t * 16 + q
+                        nc.vector.tensor_scalar(
+                            out=tl[:, t, a:z],
+                            in0=tl[:, t, a:z],
+                            scalar1=mtab[:, idx : idx + 1],
+                            scalar2=None,
+                            op0=mult,
+                        )
 
         def emit_masks_through(s, gp, si):
             want = 0
@@ -129,23 +164,25 @@ def tile_featureembed_kernel(tc, x, mask, W, b, out):
 
         def regroup(j, subs=None):
             s, gp, c = units[j]
-            width = 8 if s < 2 else 4
-            ncol = 64 * width
+            quads = (2 * c, 2 * c + 1) if s < 2 else (c,)
             if j not in grp_of:
-                grp_of[j] = grpp.tile([P, ncol, 4], BF16, name="grp", tag="grp", align_bytes=64)
-            dst_v = grp_of[j][:].rearrange("p (e i) t -> p e t i", i=width)
+                grp_of[j] = grpp.tile(
+                    [P, 256 * len(quads), 4], BF16, name="grp", tag="grp", align_bytes=64
+                )
             for si in range(len(seg_cols[(s, gp)])):
                 if subs is None or si in subs:
                     emit_masks_through(s, gp, si)
                     c0, c1 = seg_cols[(s, gp)][si]
-                    src = raw[(s, gp, si)][:].rearrange(
-                        "p t (e o i) -> p o e t i", o=16 // width, i=width
-                    )[:, c]
-                    dst = dst_v[:, c0 // 16 - 64 * s : c1 // 16 - 64 * s]
-                    if j in V_UNITS:
-                        nc.vector.tensor_copy(out=dst, in_=src)
-                    else:
-                        nc.scalar.copy(out=dst, in_=src)
+                    src_v = raw[(s, gp, si)][:].rearrange("p t (e q i) -> p q e t i", q=4, i=4)
+                    for h in range(len(quads)):
+                        dst_v = grp_of[j][:, 256 * h : 256 * h + 256, :].rearrange(
+                            "p (e i) t -> p e t i", i=4
+                        )
+                        dst = dst_v[:, c0 // 16 - 64 * s : c1 // 16 - 64 * s]
+                        if j in V_UNITS:
+                            nc.vector.tensor_copy(out=dst, in_=src_v[:, quads[h]])
+                        else:
+                            nc.scalar.copy(out=dst, in_=src_v[:, quads[h]])
 
         def quantise(j):
             s, gp, c = units[j]
@@ -203,27 +240,37 @@ def tile_featureembed_kernel(tc, x, mask, W, b, out):
             st["ex"] += 1
             st["open"] -= 1
             s, c, ct = key
+            es = slice(64 * s, 64 * s + 64)
             if s < 2:
                 if s == 0:
                     o_sb[(c, ct)] = outp.tile([P, 8, 192], F32, name="o%d_%d" % (c, ct))
                 nc.vector.tensor_tensor(
-                    out=o_sb[(c, ct)][:, :, 64 * s : 64 * s + 64],
-                    in0=acc[key][:].rearrange("p (e i) -> p i e", i=8),
-                    in1=bias_v8[:, c, :, 64 * s : 64 * s + 64],
+                    out=o_sb[(c, ct)][:, :, es].rearrange("p (h i) e -> p h i e", h=2),
+                    in0=acc[key][:].rearrange("p (h e i) -> p h i e", h=2, i=4),
+                    in1=bias_pe[:, 8 * c : 8 * c + 8, es].rearrange("p (h i) e -> p h i e", h=2),
                     op=add,
                 )
             else:
                 rows = slice(4 * (c % 2), 4 * (c % 2) + 4)
                 ot = o_sb[(c // 2, ct)]
                 nc.vector.tensor_tensor(
-                    out=ot[:, rows, 128:192],
+                    out=ot[:, rows, es],
                     in0=acc[key][:].rearrange("p (e i) -> p i e", i=4),
-                    in1=bias_v4[:, c, :, 128:192],
+                    in1=bias_pe[:, 4 * c : 4 * c + 4, es],
                     op=add,
                 )
                 nc.sync.dma_start(
                     out=out[ct * P : (ct + 1) * P, 4 * c : 4 * c + 4, :], in_=ot[:, rows, :]
                 )
+
+        def x_quant(item):
+            xg, pr, gp = item
+            cs = slice(pr * 256, (pr + 1) * 256)
+            nc.vector.quantize_mx(
+                out=xq[:, gp, cs].bitcast(FP8X4),
+                scales=xs[:, gp, cs],
+                in_=xg[:].rearrange("p c t -> p (c t)"),
+            )
 
         def x_block():
             flush_q()
@@ -247,15 +294,6 @@ def tile_featureembed_kernel(tc, x, mask, W, b, out):
             st["xdone"] = True
             flush_mm()
 
-        def x_quant(item):
-            xg, pr, gp = item
-            cs = slice(pr * 256, (pr + 1) * 256)
-            nc.vector.quantize_mx(
-                out=xq[:, gp, cs].bitcast(FP8X4),
-                scales=xs[:, gp, cs],
-                in_=xg[:].rearrange("p c t -> p (c t)"),
-            )
-
         for si in range(len(seg_cols[(0, 0)])):
             regroup(0, (si,))
             regroup(1, (si,))
@@ -276,6 +314,10 @@ def tile_featureembed_kernel(tc, x, mask, W, b, out):
                     pend_q.append(j)
                     part_a = units[j][0] < 2
                     emit_masks(A_MASKS if part_a else B_MASKS)
+                    if j == BIAS_SLOT:
+                        nc.vector.tensor_copy(
+                            out=bias_pe[:], in_=bias_sb[:].rearrange("p (e q) -> p q e", q=16)
+                        )
                     flush_mm()
                     for n in range(A_EXITS if part_a else B_EXITS):
                         emit_exit()

@@ -16,14 +16,14 @@ P = 128
 PASSES = 4
 QW = 192
 MANUAL = False
-AND_MASK = True
+AND_MASK = False
 
 LOAD_ORDER = ((0, 0), (0, 1), "x0", "x1", (0, 2), (0, 3), (1, 0), "bias", (1, 1), (1, 2), (1, 3), (2, 0), (2, 1), (2, 2), (2, 3))
 SUBS = {(0, 0): ((0, 384), (384, 1024))}
-V_UNITS = ()
-HEAD_MASKS = 2
-X_MASKS = 0
-A_MASKS = 1
+V_UNITS = (5, 18, 23, 28)
+HEAD_MASKS = 24
+X_MASKS = 3
+A_MASKS = 16
 B_MASKS = 0
 A_EXITS = 2
 B_EXITS = 2

@@ -20,7 +20,7 @@ AND_MASK = False
 
 LOAD_ORDER = ((0, 0), (0, 1), "x0", "x1", (0, 2), (0, 3), (1, 0), "bias", (1, 1), (1, 2), (1, 3), (2, 0), (2, 1), (2, 2), (2, 3))
 SUBS = {(0, 0): ((0, 384), (384, 1024))}
-V_UNITS = (5, 18, 23, 28)
+V_UNITS = (5, 11, 18, 21, 24, 27, 30)
 HEAD_MASKS = 24
 X_MASKS = 3
 A_MASKS = 16

@@ -18,9 +18,9 @@ QW = 192
 MANUAL = False
 AND_MASK = False
 
-LOAD_ORDER = ((0, 0), (0, 1), "x0", "x1", (0, 2), (0, 3), (1, 0), "bias", (1, 1), (1, 2), (1, 3), (2, 0), (2, 1), (2, 2), (2, 3))
+LOAD_ORDER = ((0, 0), (0, 1), "bias", "x0", "x1", (0, 2), (0, 3), (1, 0), (1, 1), (1, 2), (1, 3), (2, 0), (2, 1), (2, 2), (2, 3))
 SUBS = {(0, 0): ((0, 384), (384, 1024))}
-V_UNITS = (5, 11, 18, 21, 24, 27, 30)
+V_UNITS = (5, 18, 23, 28)
 HEAD_MASKS = 24
 X_MASKS = 3
 A_MASKS = 16
@@ -30,7 +30,7 @@ B_EXITS = 2
 GRP_BUFS = 5
 CODE_BUFS = 8
 XG_BUFS = 3
-BIAS_SLOT = 6
+BIAS_SLOT = 3
 
 
 def tile_featureembed_kernel(tc, x, mask, W, b, out):

@@ -7,7 +7,6 @@ FLOPS = 2 * 512 * 2048 * 3072
 
 BF16 = mybir.dt.bfloat16
 F32 = mybir.dt.float32
-I32 = mybir.dt.int32
 U32 = mybir.dt.uint32
 U8 = mybir.dt.uint8
 FP8X4 = mybir.dt.float8_e4m3fn_x4
@@ -15,11 +14,14 @@ FP8X4 = mybir.dt.float8_e4m3fn_x4
 P = 128
 PASSES = 4
 QW = 192
-MANUAL = False
-AND_MASK = False
 
-LOAD_ORDER = ((0, 0), (0, 1), "bias", "x0", "x1", (0, 2), (0, 3), (1, 0), (1, 1), (1, 2), (1, 3), (2, 0), (2, 1), (2, 2), (2, 3))
-SUBS = {(0, 0): ((0, 384), (384, 1024))}
+LOAD_ORDER = (
+    ("w", 0, 0, 384), ("w", 0, 384, 1024), ("w", 1, 0, 1024), ("b",), ("x", 0), ("x", 1),
+    ("w", 2, 0, 1024), ("w", 3, 0, 1024),
+    ("w", 0, 1024, 2048), ("w", 1, 1024, 2048), ("w", 2, 1024, 2048), ("w", 3, 1024, 2048),
+    ("w", 0, 2048, 3072), ("w", 1, 2048, 3072), ("w", 2, 2048, 3072), ("w", 3, 2048, 3072),
+)
+HEAD_E = ((0, 24), (24, 64))
 V_UNITS = (5, 18, 23, 28)
 HEAD_MASKS = 24
 X_MASKS = 3
@@ -31,6 +33,7 @@ GRP_BUFS = 5
 CODE_BUFS = 8
 XG_BUFS = 3
 BIAS_SLOT = 3
+PERMUTE_BIAS = True
 
 
 def tile_featureembed_kernel(tc, x, mask, W, b, out):
@@ -38,8 +41,6 @@ def tile_featureembed_kernel(tc, x, mask, W, b, out):
     mult = mybir.AluOpType.mult
     add = mybir.AluOpType.add
     with ExitStack() as ctx:
-        if MANUAL:
-            ctx.enter_context(tc.manual_schedule())
         const = ctx.enter_context(tc.tile_pool(name="const", bufs=1))
         rawp = ctx.enter_context(tc.tile_pool(name="raw", bufs=1))
         grpp = ctx.enter_context(tc.tile_pool(name="grp", bufs=GRP_BUFS))
@@ -56,51 +57,36 @@ def tile_featureembed_kernel(tc, x, mask, W, b, out):
         w_view = W.rearrange("(g p t) j -> g p t j", g=PASSES, p=P, t=4)
         x_view = x.rearrange("(a c p) g -> a p c g", a=2, c=2, p=P)
         bias_sb = const.tile([P, 3072], BF16, name="bias_sb")
-        bias_pe = const.tile([P, 16, 192], BF16, name="bias_pe")
         raw = {}
+        for gp in range(PASSES):
+            raw[gp] = rawp.tile([P, 4, 3072], BF16, name="raw%d" % gp)
         x_sb = {}
-        seg_cols = {}
         mask_queue = []
         for item in LOAD_ORDER:
-            if item == "x0" or item == "x1":
-                pr = 0 if item == "x0" else 1
+            if item[0] == "x":
+                pr = item[1]
                 x_sb[pr] = const.tile([P, 2, 2048], BF16, name="x_sb%d" % pr)
                 nc.sync.dma_start(out=x_sb[pr][:], in_=x_view[pr])
-            elif item == "bias":
+            elif item[0] == "b":
                 nc.sync.dma_start(out=bias_sb[:], in_=b.partition_broadcast(P))
             else:
-                s, gp = item
-                seg_cols[item] = SUBS.get(item, ((1024 * s, 1024 * s + 1024),))
-                for si in range(len(seg_cols[item])):
-                    c0, c1 = seg_cols[item][si]
-                    tl = rawp.tile([P, 4, c1 - c0], BF16, name="raw%d_%d_%d" % (s, gp, si))
-                    nc.sync.dma_start(out=tl[:], in_=w_view[gp][:, :, c0:c1])
-                    raw[(s, gp, si)] = tl
-                    if AND_MASK:
-                        qa = (c0 + QW - 1) // QW
-                        qz = c1 // QW
-                        if c0 < qa * QW:
-                            mask_queue.append((s, gp, si, qa - 1, qa, c0, qa * QW))
-                        mask_queue.append((s, gp, si, qa, qz, qa * QW, qz * QW))
-                        if qz * QW < c1:
-                            mask_queue.append((s, gp, si, qz, qz + 1, qz * QW, c1))
-                    else:
-                        for q in range(c0 // QW, (c1 - 1) // QW + 1):
-                            for t in range(4):
-                                mask_queue.append((s, gp, si, q, t))
+                gp, c0, c1 = item[1:4]
+                nc.sync.dma_start(out=raw[gp][:, :, c0:c1], in_=w_view[gp][:, :, c0:c1])
+                for q in range(c0 // QW, (c1 - 1) // QW + 1):
+                    for t in range(4):
+                        mask_queue.append((gp, q, t, max(c0, q * QW), min(c1, q * QW + QW)))
 
         ident = const.tile([P, P], F32, name="ident")
         make_identity(nc, ident[:])
-        if AND_MASK:
-            mtab = const.tile([P, PASSES * 64], I32, name="mtab")
-            nc.vector.tensor_scalar(
-                out=mtab[:], in0=mask_sb[:], scalar1=-1.0, scalar2=None, op0=mult
-            )
-        else:
-            mtab = const.tile([P, PASSES * 64], F32, name="mtab")
-            nc.vector.tensor_copy(out=mtab[:], in_=mask_sb[:])
+        mtab = const.tile([P, PASSES * 64], F32, name="mtab")
+        nc.vector.tensor_copy(out=mtab[:], in_=mask_sb[:])
         xq = const.tile([P, PASSES, 512], U32, name="xq", align_bytes=64)
         xs = const.tile([P, PASSES, 512], U8, name="xs", align_bytes=64)
+        if PERMUTE_BIAS:
+            bias_pe = const.tile([P, 16, 192], BF16, name="bias_pe")
+            bias_v = bias_pe[:].rearrange("p (q i) e -> p q i e", i=4)
+        else:
+            bias_v = bias_sb[:].rearrange("p (e q i) -> p q i e", q=4, i=4)
 
         units = []
         for s in range(2):
@@ -111,7 +97,7 @@ def tile_featureembed_kernel(tc, x, mask, W, b, out):
             for gp in range(PASSES):
                 units.append((2, gp, bq))
 
-        st = {"mi": 0, "xdone": False, "q": 0, "mm": 0, "ex": 0, "open": 0, "slot": 0}
+        st = {"mi": 0, "xdone": False, "q": 0, "mm": 0, "ex": 0, "open": 0}
         pend_q = []
         pend_mm = []
         exit_q = []
@@ -123,66 +109,49 @@ def tile_featureembed_kernel(tc, x, mask, W, b, out):
         def emit_masks(k):
             for n in range(k):
                 if st["mi"] < len(mask_queue):
-                    item = mask_queue[st["mi"]]
+                    gp, q, t, a, z = mask_queue[st["mi"]]
                     st["mi"] += 1
-                    s, gp, si = item[0:3]
-                    c0, c1 = seg_cols[(s, gp)][si]
-                    tl = raw[(s, gp, si)]
-                    if AND_MASK:
-                        q0, q1, a, z = item[3:7]
-                        words = tl[:].bitcast(I32)[:, :, (a - c0) // 2 : (z - c0) // 2]
-                        tab = mtab[:, gp * 64 : gp * 64 + 64].rearrange("p (t q) -> p t q", t=4)
-                        if q1 - q0 > 1:
-                            words = words.rearrange("p t (q w) -> p t q w", q=q1 - q0)
-                            sel = tab[:, :, q0:q1].unsqueeze(3).to_broadcast(
-                                [P, 4, q1 - q0, QW // 2]
-                            )
-                        else:
-                            sel = tab[:, :, q0:q1].to_broadcast([P, 4, (z - a) // 2])
-                        nc.vector.tensor_tensor(
-                            out=words, in0=words, in1=sel, op=mybir.AluOpType.bitwise_and
-                        )
-                    else:
-                        q, t = item[3:5]
-                        a = max(c0, q * QW) - c0
-                        z = min(c1, q * QW + QW) - c0
-                        idx = gp * 64 + t * 16 + q
-                        nc.vector.tensor_scalar(
-                            out=tl[:, t, a:z],
-                            in0=tl[:, t, a:z],
-                            scalar1=mtab[:, idx : idx + 1],
-                            scalar2=None,
-                            op0=mult,
-                        )
+                    idx = gp * 64 + t * 16 + q
+                    seg = raw[gp][:, t, a:z]
+                    nc.vector.tensor_scalar(
+                        out=seg, in0=seg, scalar1=mtab[:, idx : idx + 1], scalar2=None, op0=mult
+                    )
 
-        def emit_masks_through(s, gp, si):
+        def emit_masks_through(gp, c_hi):
             want = 0
             for n in range(len(mask_queue)):
-                if mask_queue[n][0:3] == (s, gp, si):
+                if mask_queue[n][0] == gp and mask_queue[n][3] < c_hi:
                     want = n + 1
             emit_masks(max(0, want - st["mi"]))
 
-        def regroup(j, subs=None):
+        def regroup(j, e_range=(0, 64)):
             s, gp, c = units[j]
             quads = (2 * c, 2 * c + 1) if s < 2 else (c,)
             if j not in grp_of:
                 grp_of[j] = grpp.tile(
                     [P, 256 * len(quads), 4], BF16, name="grp", tag="grp", align_bytes=64
                 )
-            for si in range(len(seg_cols[(s, gp)])):
-                if subs is None or si in subs:
-                    emit_masks_through(s, gp, si)
-                    c0, c1 = seg_cols[(s, gp)][si]
-                    src_v = raw[(s, gp, si)][:].rearrange("p t (e q i) -> p q e t i", q=4, i=4)
-                    for h in range(len(quads)):
-                        dst_v = grp_of[j][:, 256 * h : 256 * h + 256, :].rearrange(
-                            "p (e i) t -> p e t i", i=4
-                        )
-                        dst = dst_v[:, c0 // 16 - 64 * s : c1 // 16 - 64 * s]
-                        if j in V_UNITS:
-                            nc.vector.tensor_copy(out=dst, in_=src_v[:, quads[h]])
-                        else:
-                            nc.scalar.copy(out=dst, in_=src_v[:, quads[h]])
+            e0, e1 = e_range
+            emit_masks_through(gp, 1024 * s + 16 * e1)
+            src_v = raw[gp][:, :, 1024 * s : 1024 * s + 1024].rearrange(
+                "p t (e q i) -> p q e t i", q=4, i=4
+            )
+            if s < 2:
+                pairs = (
+                    (
+                        grp_of[j][:].rearrange("p (e i) t -> p e t i", i=8),
+                        raw[gp][:, :, 1024 * s : 1024 * s + 1024].rearrange(
+                            "p t (e o i) -> p o e t i", o=2, i=8
+                        )[:, c],
+                    ),
+                )
+            else:
+                pairs = ((grp_of[j][:].rearrange("p (e i) t -> p e t i", i=4), src_v[:, c]),)
+            for dst_v, src_q in pairs:
+                if j in V_UNITS:
+                    nc.vector.tensor_copy(out=dst_v[:, e0:e1], in_=src_q[:, e0:e1])
+                else:
+                    nc.scalar.copy(out=dst_v[:, e0:e1], in_=src_q[:, e0:e1])
 
         def quantise(j):
             s, gp, c = units[j]
@@ -245,9 +214,9 @@ def tile_featureembed_kernel(tc, x, mask, W, b, out):
                 if s == 0:
                     o_sb[(c, ct)] = outp.tile([P, 8, 192], F32, name="o%d_%d" % (c, ct))
                 nc.vector.tensor_tensor(
-                    out=o_sb[(c, ct)][:, :, es].rearrange("p (h i) e -> p h i e", h=2),
-                    in0=acc[key][:].rearrange("p (h e i) -> p h i e", h=2, i=4),
-                    in1=bias_pe[:, 8 * c : 8 * c + 8, es].rearrange("p (h i) e -> p h i e", h=2),
+                    out=o_sb[(c, ct)][:, :, es],
+                    in0=acc[key][:].rearrange("p (e i) -> p i e", i=8),
+                    in1=bias_pe[:, 8 * c : 8 * c + 8, es],
                     op=add,
                 )
             else:
@@ -256,7 +225,7 @@ def tile_featureembed_kernel(tc, x, mask, W, b, out):
                 nc.vector.tensor_tensor(
                     out=ot[:, rows, es],
                     in0=acc[key][:].rearrange("p (e i) -> p i e", i=4),
-                    in1=bias_pe[:, 4 * c : 4 * c + 4, es],
+                    in1=bias_v[:, c, :, es],
                     op=add,
                 )
                 nc.sync.dma_start(
@@ -294,11 +263,11 @@ def tile_featureembed_kernel(tc, x, mask, W, b, out):
             st["xdone"] = True
             flush_mm()
 
-        for si in range(len(seg_cols[(0, 0)])):
-            regroup(0, (si,))
-            regroup(1, (si,))
+        for si in range(2):
+            regroup(0, HEAD_E[si])
+            regroup(1, HEAD_E[si])
             if si == 0:
-                emit_masks_through(0, 0, 1)
+                emit_masks_through(0, 1024)
         emit_masks(HEAD_MASKS)
         pend_q.append(0)
         pend_q.append(1)
@@ -314,7 +283,7 @@ def tile_featureembed_kernel(tc, x, mask, W, b, out):
                     pend_q.append(j)
                     part_a = units[j][0] < 2
                     emit_masks(A_MASKS if part_a else B_MASKS)
-                    if j == BIAS_SLOT:
+                    if j == BIAS_SLOT and PERMUTE_BIAS:
                         nc.vector.tensor_copy(
                             out=bias_pe[:], in_=bias_sb[:].rearrange("p (e q) -> p q e", q=16)
                         )

@@ -22,13 +22,16 @@ LOAD_ORDER = (
     ("w", 0, 2048, 3072), ("w", 1, 2048, 3072), ("w", 2, 2048, 3072), ("w", 3, 2048, 3072),
 )
 HEAD_E = ((0, 24), (24, 64))
-V_UNITS = (5, 18, 23, 28)
+V_UNITS = ()
+G_CHAIN = (7, 9, 15, 19, 22, 26, 30)
+G_FIRST_AT = 6
+WINDOW = 4
 HEAD_MASKS = 24
 X_MASKS = 3
 A_MASKS = 16
 B_MASKS = 0
-A_EXITS = 2
-B_EXITS = 2
+A_EXITS = 0
+B_EXITS = 0
 GRP_BUFS = 5
 CODE_BUFS = 8
 XG_BUFS = 3
@@ -44,6 +47,7 @@ def tile_featureembed_kernel(tc, x, mask, W, b, out):
         const = ctx.enter_context(tc.tile_pool(name="const", bufs=1))
         rawp = ctx.enter_context(tc.tile_pool(name="raw", bufs=1))
         grpp = ctx.enter_context(tc.tile_pool(name="grp", bufs=GRP_BUFS))
+        ggp = ctx.enter_context(tc.tile_pool(name="gg", bufs=1))
         xgp = ctx.enter_context(tc.tile_pool(name="xg", bufs=XG_BUFS))
         codep = ctx.enter_context(tc.tile_pool(name="code", bufs=CODE_BUFS))
         outp = ctx.enter_context(tc.tile_pool(name="outp", bufs=1))
@@ -102,6 +106,7 @@ def tile_featureembed_kernel(tc, x, mask, W, b, out):
         pend_mm = []
         exit_q = []
         grp_of = {}
+        g_of = {}
         codes = {}
         acc = {}
         o_sb = {}
@@ -129,9 +134,13 @@ def tile_featureembed_kernel(tc, x, mask, W, b, out):
             quads = (2 * c, 2 * c + 1) if s < 2 else (c,)
             if j not in grp_of:
                 grp_of[j] = grpp.tile(
-                    [P, 256 * len(quads), 4], BF16, name="grp", tag="grp", align_bytes=64
+                    [P, 256 if j in G_CHAIN else 256 * len(quads), 4],
+                    BF16,
+                    name="grp",
+                    tag="grp",
+                    align_bytes=64,
                 )
-            e0, e1 = e_range
+            e0, e1 = (0, 32) if j in G_CHAIN else e_range
             emit_masks_through(gp, 1024 * s + 16 * e1)
             src_v = raw[gp][:, :, 1024 * s : 1024 * s + 1024].rearrange(
                 "p t (e q i) -> p q e t i", q=4, i=4
@@ -153,17 +162,50 @@ def tile_featureembed_kernel(tc, x, mask, W, b, out):
                 else:
                     nc.scalar.copy(out=dst_v[:, e0:e1], in_=src_q[:, e0:e1])
 
+        def regroup_g(j):
+            s, gp, c = units[j]
+            g_of[j] = ggp.tile([P, 256, 4], BF16, name="gg", tag="gg", align_bytes=64)
+            emit_masks_through(gp, 1024 * s + 1024)
+            part = raw[gp][:, :, 1024 * s : 1024 * s + 1024]
+            if s < 2:
+                src_g = part.rearrange("p t (e o i) -> p o e t i", o=2, i=8)[:, c, 32:64]
+                dst_g = g_of[j][:].rearrange("p (e i) t -> p e t i", i=8)
+            else:
+                src_g = part.rearrange("p t (e q i) -> p q e t i", q=4, i=4)[:, c]
+                dst_g = g_of[j][:].rearrange("p (e i) t -> p e t i", i=4)
+            nc.gpsimd.tensor_scalar(
+                out=dst_g, in0=src_g, scalar1=1.0, scalar2=0.0, op0=mult, op1=add
+            )
+
         def quantise(j):
             s, gp, c = units[j]
             ncol = 512 if s < 2 else 256
             wq = codep.tile([P, ncol], U32, name="wq", tag="wq", align_bytes=64)
             ws = codep.tile([P, ncol], U8, name="ws", tag="ws", align_bytes=64)
-            nc.vector.quantize_mx(
-                out=wq[:].bitcast(FP8X4),
-                scales=ws[:],
-                in_=grp_of[j][:].rearrange("p c t -> p (c t)"),
-            )
             codes[j] = (wq, ws)
+            if j not in G_CHAIN:
+                nc.vector.quantize_mx(
+                    out=wq[:].bitcast(FP8X4),
+                    scales=ws[:],
+                    in_=grp_of[j][:].rearrange("p c t -> p (c t)"),
+                )
+                return
+            if s < 2:
+                nc.vector.quantize_mx(
+                    out=wq[:, 0:256].bitcast(FP8X4),
+                    scales=ws[:, 0:256],
+                    in_=grp_of[j][:].rearrange("p c t -> p (c t)"),
+                )
+            nc.vector.quantize_mx(
+                out=wq[:, ncol - 256 : ncol].bitcast(FP8X4),
+                scales=ws[:, ncol - 256 : ncol],
+                in_=g_of[j][:].rearrange("p c t -> p (c t)"),
+            )
+            k = G_CHAIN.index(j)
+            if k + 1 < len(G_CHAIN):
+                regroup_g(G_CHAIN[k + 1])
+            for n in range(WINDOW):
+                emit_exit()
 
         def flush_q():
             while st["q"] < len(pend_q):
@@ -274,8 +316,12 @@ def tile_featureembed_kernel(tc, x, mask, W, b, out):
         for j in (2, 3, "X") + tuple(range(4, 32)):
             if j == "X":
                 x_block()
+            elif j in G_CHAIN and units[j][0] == 2:
+                pend_q.append(j)
             else:
                 regroup(j)
+                if j == G_FIRST_AT:
+                    regroup_g(G_CHAIN[0])
                 if j in V_UNITS:
                     pend_q.append(j)
                 else:

@@ -23,8 +23,11 @@ LOAD_ORDER = (
 )
 HEAD_E = ((0, 24), (24, 64))
 V_UNITS = ()
-G_CHAIN = (7, 9, 15, 19, 22, 26, 30)
-G_FIRST_AT = 6
+CHAIN = {
+    7: ("scalar", 32), 9: ("gpsimd", 32), 15: ("gpsimd", 32), 18: ("gpsimd", 0),
+    20: ("gpsimd", 32), 24: ("gpsimd", 32), 28: ("gpsimd", 32),
+}
+CHAIN_ORDER = tuple(sorted(CHAIN))
 WINDOW = 4
 HEAD_MASKS = 24
 X_MASKS = 3
@@ -132,15 +135,15 @@ def tile_featureembed_kernel(tc, x, mask, W, b, out):
         def regroup(j, e_range=(0, 64)):
             s, gp, c = units[j]
             quads = (2 * c, 2 * c + 1) if s < 2 else (c,)
+            e0, e1 = (0, CHAIN[j][1]) if j in CHAIN else e_range
             if j not in grp_of:
                 grp_of[j] = grpp.tile(
-                    [P, 256 if j in G_CHAIN else 256 * len(quads), 4],
+                    [P, (e1 if j in CHAIN else 64) * 4 * len(quads), 4],
                     BF16,
                     name="grp",
                     tag="grp",
                     align_bytes=64,
                 )
-            e0, e1 = (0, 32) if j in G_CHAIN else e_range
             emit_masks_through(gp, 1024 * s + 16 * e1)
             src_v = raw[gp][:, :, 1024 * s : 1024 * s + 1024].rearrange(
                 "p t (e q i) -> p q e t i", q=4, i=4
@@ -162,20 +165,24 @@ def tile_featureembed_kernel(tc, x, mask, W, b, out):
                 else:
                     nc.scalar.copy(out=dst_v[:, e0:e1], in_=src_q[:, e0:e1])
 
-        def regroup_g(j):
+        def regroup_chain(j):
             s, gp, c = units[j]
-            g_of[j] = ggp.tile([P, 256, 4], BF16, name="gg", tag="gg", align_bytes=64)
+            engine, e_lo = CHAIN[j]
+            iw = 8 if s < 2 else 4
+            g_of[j] = ggp.tile([P, (64 - e_lo) * iw, 4], BF16, name="gg", tag="gg", align_bytes=64)
             emit_masks_through(gp, 1024 * s + 1024)
             part = raw[gp][:, :, 1024 * s : 1024 * s + 1024]
             if s < 2:
-                src_g = part.rearrange("p t (e o i) -> p o e t i", o=2, i=8)[:, c, 32:64]
-                dst_g = g_of[j][:].rearrange("p (e i) t -> p e t i", i=8)
+                src_g = part.rearrange("p t (e o i) -> p o e t i", o=2, i=8)[:, c, e_lo:64]
             else:
-                src_g = part.rearrange("p t (e q i) -> p q e t i", q=4, i=4)[:, c]
-                dst_g = g_of[j][:].rearrange("p (e i) t -> p e t i", i=4)
-            nc.gpsimd.tensor_scalar(
-                out=dst_g, in0=src_g, scalar1=1.0, scalar2=0.0, op0=mult, op1=add
-            )
+                src_g = part.rearrange("p t (e q i) -> p q e t i", q=4, i=4)[:, c, e_lo:64]
+            dst_g = g_of[j][:].rearrange("p (e i) t -> p e t i", i=iw)
+            if engine == "scalar":
+                nc.scalar.copy(out=dst_g, in_=src_g)
+            else:
+                nc.gpsimd.tensor_scalar(
+                    out=dst_g, in0=src_g, scalar1=1.0, scalar2=0.0, op0=mult, op1=add
+                )
 
         def quantise(j):
             s, gp, c = units[j]
@@ -183,27 +190,28 @@ def tile_featureembed_kernel(tc, x, mask, W, b, out):
             wq = codep.tile([P, ncol], U32, name="wq", tag="wq", align_bytes=64)
             ws = codep.tile([P, ncol], U8, name="ws", tag="ws", align_bytes=64)
             codes[j] = (wq, ws)
-            if j not in G_CHAIN:
+            if j not in CHAIN:
                 nc.vector.quantize_mx(
                     out=wq[:].bitcast(FP8X4),
                     scales=ws[:],
                     in_=grp_of[j][:].rearrange("p c t -> p (c t)"),
                 )
                 return
-            if s < 2:
+            cut = CHAIN[j][1] * (8 if s < 2 else 4)
+            if cut > 0:
                 nc.vector.quantize_mx(
-                    out=wq[:, 0:256].bitcast(FP8X4),
-                    scales=ws[:, 0:256],
+                    out=wq[:, 0:cut].bitcast(FP8X4),
+                    scales=ws[:, 0:cut],
                     in_=grp_of[j][:].rearrange("p c t -> p (c t)"),
                 )
             nc.vector.quantize_mx(
-                out=wq[:, ncol - 256 : ncol].bitcast(FP8X4),
-                scales=ws[:, ncol - 256 : ncol],
+                out=wq[:, cut:ncol].bitcast(FP8X4),
+                scales=ws[:, cut:ncol],
                 in_=g_of[j][:].rearrange("p c t -> p (c t)"),
             )
-            k = G_CHAIN.index(j)
-            if k + 1 < len(G_CHAIN):
-                regroup_g(G_CHAIN[k + 1])
+            k = CHAIN_ORDER.index(j)
+            if k + 1 < len(CHAIN_ORDER):
+                regroup_chain(CHAIN_ORDER[k + 1])
             for n in range(WINDOW):
                 emit_exit()
 
@@ -316,12 +324,12 @@ def tile_featureembed_kernel(tc, x, mask, W, b, out):
         for j in (2, 3, "X") + tuple(range(4, 32)):
             if j == "X":
                 x_block()
-            elif j in G_CHAIN and units[j][0] == 2:
+            elif j in CHAIN and CHAIN[j][1] == 0:
                 pend_q.append(j)
             else:
                 regroup(j)
-                if j == G_FIRST_AT:
-                    regroup_g(G_CHAIN[0])
+                if j == CHAIN_ORDER[0]:
+                    regroup_chain(j)
                 if j in V_UNITS:
                     pend_q.append(j)
                 else:

@@ -22,7 +22,7 @@ LOAD_ORDER = (
     ("w", 0, 2048, 3072), ("w", 1, 2048, 3072), ("w", 2, 2048, 3072), ("w", 3, 2048, 3072),
 )
 HEAD_E = ((0, 24), (24, 64))
-V_UNITS = ()
+V_UNITS = (5,)
 CHAIN = {
     7: ("scalar", 32), 9: ("gpsimd", 32), 15: ("gpsimd", 32), 18: ("gpsimd", 0),
     20: ("gpsimd", 32), 24: ("gpsimd", 32), 28: ("gpsimd", 32),

@@ -18,8 +18,8 @@ QW = 192
 LOAD_ORDER = (
     ("w", 0, 0, 384), ("w", 0, 384, 1024), ("w", 1, 0, 1024), ("b",), ("x", 0), ("x", 1),
     ("w", 2, 0, 1024), ("w", 3, 0, 1024),
-    ("w", 0, 1024, 2048), ("w", 1, 1024, 2048), ("w", 2, 1024, 2048), ("w", 3, 1024, 2048),
-    ("w", 0, 2048, 3072), ("w", 1, 2048, 3072), ("w", 2, 2048, 3072), ("w", 3, 2048, 3072),
+    ("w", 0, 1024, 2112), ("w", 1, 1024, 2112), ("w", 2, 1024, 2112), ("w", 3, 1024, 2112),
+    ("w", 0, 2112, 3072), ("w", 1, 2112, 3072), ("w", 2, 2112, 3072), ("w", 3, 2112, 3072),
 )
 HEAD_E = ((0, 24), (24, 64))
 V_UNITS = (5,)

@@ -16,7 +16,7 @@ PASSES = 4
 QW = 192
 
 LOAD_ORDER = (
-    ("w", 0, 0, 384), ("w", 0, 384, 1024), ("w", 1, 0, 1024), ("b",), ("x", 0), ("x", 1),
+    ("w", 0, 0, 384), ("b",), ("w", 0, 384, 1024), ("w", 1, 0, 1024), ("x", 0), ("x", 1),
     ("w", 2, 0, 1024), ("w", 3, 0, 1024),
     ("w", 0, 1024, 2112), ("w", 1, 1024, 2112), ("w", 2, 1024, 2112), ("w", 3, 1024, 2112),
     ("w", 0, 2112, 3072), ("w", 1, 2112, 3072), ("w", 2, 2112, 3072), ("w", 3, 2112, 3072),
@@ -39,7 +39,6 @@ GRP_BUFS = 5
 CODE_BUFS = 8
 XG_BUFS = 3
 BIAS_SLOT = 3
-PERMUTE_BIAS = True
 
 
 def tile_featureembed_kernel(tc, x, mask, W, b, out):
@@ -63,7 +62,9 @@ def tile_featureembed_kernel(tc, x, mask, W, b, out):
         )
         w_view = W.rearrange("(g p t) j -> g p t j", g=PASSES, p=P, t=4)
         x_view = x.rearrange("(a c p) g -> a p c g", a=2, c=2, p=P)
-        bias_sb = const.tile([P, 3072], BF16, name="bias_sb")
+        b_lo = const.tile([P, 16], BF16, name="b_lo")
+        b_hi = const.tile([P, 16], BF16, name="b_hi")
+        nc.vector.memset(b_hi[:], 0.0)
         raw = {}
         for gp in range(PASSES):
             raw[gp] = rawp.tile([P, 4, 3072], BF16, name="raw%d" % gp)
@@ -75,7 +76,9 @@ def tile_featureembed_kernel(tc, x, mask, W, b, out):
                 x_sb[pr] = const.tile([P, 2, 2048], BF16, name="x_sb%d" % pr)
                 nc.sync.dma_start(out=x_sb[pr][:], in_=x_view[pr])
             elif item[0] == "b":
-                nc.sync.dma_start(out=bias_sb[:], in_=b.partition_broadcast(P))
+                b_view = b.rearrange("(e q) -> e q", q=16)
+                nc.sync.dma_start(out=b_lo[:], in_=b_view[0:128, :])
+                nc.sync.dma_start(out=b_hi[0:64, :], in_=b_view[128:192, :])
             else:
                 gp, c0, c1 = item[1:4]
                 nc.sync.dma_start(out=raw[gp][:, :, c0:c1], in_=w_view[gp][:, :, c0:c1])
@@ -85,15 +88,38 @@ def tile_featureembed_kernel(tc, x, mask, W, b, out):
 
         ident = const.tile([P, P], F32, name="ident")
         make_identity(nc, ident[:])
+        identb = const.tile([P, P], BF16, name="identb")
+        nc.gpsimd.tensor_copy(out=identb[:], in_=ident[:])
         mtab = const.tile([P, PASSES * 64], F32, name="mtab")
         nc.vector.tensor_copy(out=mtab[:], in_=mask_sb[:])
         xq = const.tile([P, PASSES, 512], U32, name="xq", align_bytes=64)
         xs = const.tile([P, PASSES, 512], U8, name="xs", align_bytes=64)
-        if PERMUTE_BIAS:
-            bias_pe = const.tile([P, 16, 192], BF16, name="bias_pe")
-            bias_v = bias_pe[:].rearrange("p (q i) e -> p q i e", i=4)
-        else:
-            bias_v = bias_sb[:].rearrange("p (e q i) -> p q i e", q=4, i=4)
+        bias_pe = const.tile([P, 16, 192], BF16, name="bias_pe")
+        bias_v = bias_pe[:].rearrange("p (q i) e -> p q i e", i=4)
+
+        def spread_bias():
+            for k in range(4):
+                pb = psum.tile([P, 4, 192], BF16, name="pb", tag="bank")
+                for i in range(4):
+                    q = 4 * k + i
+                    nc.tensor.matmul(
+                        pb[:, i, 0:128],
+                        lhsT=b_lo[:, q : q + 1].to_broadcast([P, P]),
+                        rhs=identb[:],
+                        start=True,
+                        stop=True,
+                    )
+                    nc.tensor.matmul(
+                        pb[:, i, 128:192],
+                        lhsT=b_hi[:, q : q + 1].to_broadcast([P, P]),
+                        rhs=identb[:, 0:64],
+                        start=True,
+                        stop=True,
+                    )
+                nc.scalar.copy(
+                    out=bias_pe[:, 4 * k : 4 * k + 4, :].rearrange("p q e -> p (q e)").bitcast(F32),
+                    in_=pb[:].rearrange("p q e -> p (q e)").bitcast(F32),
+                )
 
         units = []
         for s in range(2):
@@ -337,10 +363,8 @@ def tile_featureembed_kernel(tc, x, mask, W, b, out):
                     pend_q.append(j)
                     part_a = units[j][0] < 2
                     emit_masks(A_MASKS if part_a else B_MASKS)
-                    if j == BIAS_SLOT and PERMUTE_BIAS:
-                        nc.vector.tensor_copy(
-                            out=bias_pe[:], in_=bias_sb[:].rearrange("p (e q) -> p q e", q=16)
-                        )
+                    if j == BIAS_SLOT:
+                        spread_bias()
                     flush_mm()
                     for n in range(A_EXITS if part_a else B_EXITS):
                         emit_exit()

@@ -295,6 +295,11 @@ def tile_featureembed_kernel(tc, x, mask, W, b, out):
                     in1=bias_pe[:, 8 * c : 8 * c + 8, es],
                     op=add,
                 )
+                if s == 1 and c == 1:
+                    nc.sync.dma_start(
+                        out=out[ct * P : (ct + 1) * P, 12:16, 0:128],
+                        in_=o_sb[(c, ct)][:, 4:8, 0:128],
+                    )
             else:
                 rows = slice(4 * (c % 2), 4 * (c % 2) + 4)
                 ot = o_sb[(c // 2, ct)]
@@ -304,8 +309,10 @@ def tile_featureembed_kernel(tc, x, mask, W, b, out):
                     in1=bias_v[:, c, :, es],
                     op=add,
                 )
+                e_out = slice(0, 192) if c < 3 else es
                 nc.sync.dma_start(
-                    out=out[ct * P : (ct + 1) * P, 4 * c : 4 * c + 4, :], in_=ot[:, rows, :]
+                    out=out[ct * P : (ct + 1) * P, 4 * c : 4 * c + 4, e_out],
+                    in_=ot[:, rows, e_out],
                 )
 
         def x_quant(item):

@@ -22,7 +22,7 @@ LOAD_ORDER = (
     ("w", 0, 2112, 3072), ("w", 1, 2112, 3072), ("w", 2, 2112, 3072), ("w", 3, 2112, 3072),
 )
 HEAD_E = ((0, 24), (24, 64))
-V_UNITS = (5,)
+V_UNITS = (2, 3, 5)
 CHAIN = {
     7: ("scalar", 32), 9: ("gpsimd", 32), 15: ("gpsimd", 32), 18: ("gpsimd", 0),
     20: ("gpsimd", 32), 24: ("gpsimd", 32), 28: ("gpsimd", 32),
@@ -38,7 +38,6 @@ B_EXITS = 0
 GRP_BUFS = 5
 CODE_BUFS = 8
 XG_BUFS = 3
-BIAS_SLOT = 3
 
 
 def tile_featureembed_kernel(tc, x, mask, W, b, out):
@@ -352,6 +351,7 @@ def tile_featureembed_kernel(tc, x, mask, W, b, out):
             if si == 0:
                 emit_masks_through(0, 1024)
         emit_masks(HEAD_MASKS)
+        spread_bias()
         pend_q.append(0)
         pend_q.append(1)
         for j in (2, 3, "X") + tuple(range(4, 32)):
@@ -370,8 +370,6 @@ def tile_featureembed_kernel(tc, x, mask, W, b, out):
                     pend_q.append(j)
                     part_a = units[j][0] < 2
                     emit_masks(A_MASKS if part_a else B_MASKS)
-                    if j == BIAS_SLOT:
-                        spread_bias()
                     flush_mm()
                     for n in range(A_EXITS if part_a else B_EXITS):
                         emit_exit()

@@ -123,7 +123,7 @@ def tile_featureembed_kernel(tc, x, mask, W, b, out):
         units = []
         for s in range(2):
             for gp in range(PASSES):
-                for o in range(2):
+                for o in (0, 1) if s == 0 else (1, 0):
                     units.append((s, gp, o))
         for bq in range(4):
             for gp in range(PASSES):

@@ -223,22 +223,26 @@ def tile_featureembed_kernel(tc, x, mask, W, b, out):
                 )
                 return
             cut = CHAIN[j][1] * (8 if s < 2 else 4)
+            k = CHAIN_ORDER.index(j)
+            last = k + 1 == len(CHAIN_ORDER)
             if cut > 0:
                 nc.vector.quantize_mx(
                     out=wq[:, 0:cut].bitcast(FP8X4),
                     scales=ws[:, 0:cut],
                     in_=grp_of[j][:].rearrange("p c t -> p (c t)"),
                 )
+            if last:
+                for n in range(WINDOW):
+                    emit_exit()
             nc.vector.quantize_mx(
                 out=wq[:, cut:ncol].bitcast(FP8X4),
                 scales=ws[:, cut:ncol],
                 in_=g_of[j][:].rearrange("p c t -> p (c t)"),
             )
-            k = CHAIN_ORDER.index(j)
-            if k + 1 < len(CHAIN_ORDER):
+            if not last:
                 regroup_chain(CHAIN_ORDER[k + 1])
-            for n in range(WINDOW):
-                emit_exit()
+                for n in range(WINDOW):
+                    emit_exit()
 
         def flush_q():
             while st["q"] < len(pend_q):

@@ -23,6 +23,7 @@ LOAD_ORDER = (
 )
 HEAD_E = ((0, 24), (24, 64))
 V_UNITS = (2, 3, 5)
+SHARED_UNITS = (31,)
 CHAIN = {
     7: ("scalar", 32), 9: ("gpsimd", 32), 15: ("gpsimd", 32), 18: ("gpsimd", 0),
     20: ("gpsimd", 32), 24: ("gpsimd", 32), 28: ("gpsimd", 32),
@@ -185,7 +186,11 @@ def tile_featureembed_kernel(tc, x, mask, W, b, out):
             else:
                 pairs = ((grp_of[j][:].rearrange("p (e i) t -> p e t i", i=4), src_v[:, c]),)
             for dst_v, src_q in pairs:
-                if j in V_UNITS:
+                if j in SHARED_UNITS:
+                    mid = (e0 + e1) // 2
+                    nc.scalar.copy(out=dst_v[:, e0:mid], in_=src_q[:, e0:mid])
+                    nc.vector.tensor_copy(out=dst_v[:, mid:e1], in_=src_q[:, mid:e1])
+                elif j in V_UNITS:
                     nc.vector.tensor_copy(out=dst_v[:, e0:e1], in_=src_q[:, e0:e1])
                 else:
                     nc.scalar.copy(out=dst_v[:, e0:e1], in_=src_q[:, e0:e1])
@@ -300,8 +305,8 @@ def tile_featureembed_kernel(tc, x, mask, W, b, out):
                 )
                 if s == 1 and c == 1:
                     nc.sync.dma_start(
-                        out=out[ct * P : (ct + 1) * P, 12:16, 0:128],
-                        in_=o_sb[(c, ct)][:, 4:8, 0:128],
+                        out=out[ct * P : (ct + 1) * P, 8:16, 0:128],
+                        in_=o_sb[(c, ct)][:, :, 0:128],
                     )
             else:
                 rows = slice(4 * (c % 2), 4 * (c % 2) + 4)
@@ -312,7 +317,7 @@ def tile_featureembed_kernel(tc, x, mask, W, b, out):
                     in1=bias_v[:, c, :, es],
                     op=add,
                 )
-                e_out = slice(0, 192) if c < 3 else es
+                e_out = slice(0, 192) if c < 2 else es
                 nc.sync.dma_start(
                     out=out[ct * P : (ct + 1) * P, 4 * c : 4 * c + 4, e_out],
                     in_=ot[:, rows, e_out],

from contextlib import ExitStack

import concourse.mybir as mybir
from concourse.masks import make_identity

FLOPS = 2 * 512 * 2048 * 3072

BF16 = mybir.dt.bfloat16
F32 = mybir.dt.float32
U32 = mybir.dt.uint32
U8 = mybir.dt.uint8
FP8X4 = mybir.dt.float8_e4m3fn_x4

P = 128
PASSES = 4
QW = 192

LOAD_ORDER = (
    ("w", 0, 0, 384), ("b",), ("w", 0, 384, 1024), ("w", 1, 0, 1024), ("x", 0), ("x", 1),
    ("w", 2, 0, 1024), ("w", 3, 0, 1024),
    ("w", 0, 1024, 2112), ("w", 1, 1024, 2112), ("w", 2, 1024, 2112), ("w", 3, 1024, 2112),
    ("w", 0, 2112, 3072), ("w", 1, 2112, 3072), ("w", 2, 2112, 3072), ("w", 3, 2112, 3072),
)
HEAD_E = ((0, 24), (24, 64))
V_UNITS = (2, 3, 5)
SHARED_UNITS = (31,)
CHAIN = {
    7: ("scalar", 32), 9: ("gpsimd", 32), 15: ("gpsimd", 32), 18: ("gpsimd", 0),
    20: ("gpsimd", 32), 24: ("gpsimd", 32), 28: ("gpsimd", 32),
}
CHAIN_ORDER = tuple(sorted(CHAIN))
WINDOW = 4
HEAD_MASKS = 24
X_MASKS = 3
A_MASKS = 16
B_MASKS = 0
A_EXITS = 0
B_EXITS = 0
GRP_BUFS = 5
CODE_BUFS = 8
XG_BUFS = 3


def tile_featureembed_kernel(tc, x, mask, W, b, out):
    nc = tc.nc
    mult = mybir.AluOpType.mult
    add = mybir.AluOpType.add
    with ExitStack() as ctx:
        const = ctx.enter_context(tc.tile_pool(name="const", bufs=1))
        rawp = ctx.enter_context(tc.tile_pool(name="raw", bufs=1))
        grpp = ctx.enter_context(tc.tile_pool(name="grp", bufs=GRP_BUFS))
        ggp = ctx.enter_context(tc.tile_pool(name="gg", bufs=1))
        xgp = ctx.enter_context(tc.tile_pool(name="xg", bufs=XG_BUFS))
        codep = ctx.enter_context(tc.tile_pool(name="code", bufs=CODE_BUFS))
        outp = ctx.enter_context(tc.tile_pool(name="outp", bufs=1))
        psum = ctx.enter_context(tc.psum_pool(name="psum", bufs=8))

        mask_sb = const.tile([P, PASSES * 64], BF16, name="mask_sb")
        nc.sync.dma_start(
            out=mask_sb[:].rearrange("p (g c) -> p g c", g=PASSES),
            in_=mask.rearrange("(g p t) q -> p g (t q)", g=PASSES, p=P, t=4),
        )
        w_view = W.rearrange("(g p t) j -> g p t j", g=PASSES, p=P, t=4)
        x_view = x.rearrange("(a c p) g -> a p c g", a=2, c=2, p=P)
        b_lo = const.tile([P, 16], BF16, name="b_lo")
        b_hi = const.tile([P, 16], BF16, name="b_hi")
        nc.vector.memset(b_hi[:], 0.0)
        raw = {}
        for gp in range(PASSES):
            raw[gp] = rawp.tile([P, 4, 3072], BF16, name="raw%d" % gp)
        x_sb = {}
        mask_queue = []
        for item in LOAD_ORDER:
            if item[0] == "x":
                pr = item[1]
                x_sb[pr] = const.tile([P, 2, 2048], BF16, name="x_sb%d" % pr)
                nc.sync.dma_start(out=x_sb[pr][:], in_=x_view[pr])
            elif item[0] == "b":
                b_view = b.rearrange("(e q) -> e q", q=16)
                nc.sync.dma_start(out=b_lo[:], in_=b_view[0:128, :])
                nc.sync.dma_start(out=b_hi[0:64, :], in_=b_view[128:192, :])
            else:
                gp, c0, c1 = item[1:4]
                nc.sync.dma_start(out=raw[gp][:, :, c0:c1], in_=w_view[gp][:, :, c0:c1])
                for q in range(c0 // QW, (c1 - 1) // QW + 1):
                    for t in range(4):
                        mask_queue.append((gp, q, t, max(c0, q * QW), min(c1, q * QW + QW)))

        ident = const.tile([P, P], F32, name="ident")
        make_identity(nc, ident[:])
        identb = const.tile([P, P], BF16, name="identb")
        nc.gpsimd.tensor_copy(out=identb[:], in_=ident[:])
        mtab = const.tile([P, PASSES * 64], F32, name="mtab")
        nc.vector.tensor_copy(out=mtab[:], in_=mask_sb[:])
        xq = const.tile([P, PASSES, 512], U32, name="xq", align_bytes=64)
        xs = const.tile([P, PASSES, 512], U8, name="xs", align_bytes=64)
        bias_pe = const.tile([P, 16, 192], BF16, name="bias_pe")
        bias_v = bias_pe[:].rearrange("p (q i) e -> p q i e", i=4)

        def spread_bias():
            for k in range(4):
                pb = psum.tile([P, 4, 192], BF16, name="pb", tag="bank")
                for i in range(4):
                    q = 4 * k + i
                    nc.tensor.matmul(
                        pb[:, i, 0:128],
                        lhsT=b_lo[:, q : q + 1].to_broadcast([P, P]),
                        rhs=identb[:],
                        start=True,
                        stop=True,
                    )
                    nc.tensor.matmul(
                        pb[:, i, 128:192],
                        lhsT=b_hi[:, q : q + 1].to_broadcast([P, P]),
                        rhs=identb[:, 0:64],
                        start=True,
                        stop=True,
                    )
                nc.scalar.copy(
                    out=bias_pe[:, 4 * k : 4 * k + 4, :].rearrange("p q e -> p (q e)").bitcast(F32),
                    in_=pb[:].rearrange("p q e -> p (q e)").bitcast(F32),
                )

        units = []
        for s in range(2):
            for gp in range(PASSES):
                for o in (0, 1) if s == 0 else (1, 0):
                    units.append((s, gp, o))
        for bq in range(4):
            for gp in range(PASSES):
                units.append((2, gp, bq))

        st = {"mi": 0, "xdone": False, "q": 0, "mm": 0, "ex": 0, "open": 0}
        pend_q = []
        pend_mm = []
        exit_q = []
        grp_of = {}
        g_of = {}
        codes = {}
        acc = {}
        o_sb = {}

        def emit_masks(k):
            for n in range(k):
                if st["mi"] < len(mask_queue):
                    gp, q, t, a, z = mask_queue[st["mi"]]
                    st["mi"] += 1
                    idx = gp * 64 + t * 16 + q
                    seg = raw[gp][:, t, a:z]
                    nc.vector.tensor_scalar(
                        out=seg, in0=seg, scalar1=mtab[:, idx : idx + 1], scalar2=None, op0=mult
                    )

        def emit_masks_through(gp, c_hi):
            want = 0
            for n in range(len(mask_queue)):
                if mask_queue[n][0] == gp and mask_queue[n][3] < c_hi:
                    want = n + 1
            emit_masks(max(0, want - st["mi"]))

        def regroup(j, e_range=(0, 64)):
            s, gp, c = units[j]
            quads = (2 * c, 2 * c + 1) if s < 2 else (c,)
            e0, e1 = (0, CHAIN[j][1]) if j in CHAIN else e_range
            if j not in grp_of:
                grp_of[j] = grpp.tile(
                    [P, (e1 if j in CHAIN else 64) * 4 * len(quads), 4],
                    BF16,
                    name="grp",
                    tag="grp",
                    align_bytes=64,
                )
            emit_masks_through(gp, 1024 * s + 16 * e1)
            src_v = raw[gp][:, :, 1024 * s : 1024 * s + 1024].rearrange(
                "p t (e q i) -> p q e t i", q=4, i=4
            )
            if s < 2:
                pairs = (
                    (
                        grp_of[j][:].rearrange("p (e i) t -> p e t i", i=8),
                        raw[gp][:, :, 1024 * s : 1024 * s + 1024].rearrange(
                            "p t (e o i) -> p o e t i", o=2, i=8
                        )[:, c],
                    ),
                )
            else:
                pairs = ((grp_of[j][:].rearrange("p (e i) t -> p e t i", i=4), src_v[:, c]),)
            for dst_v, src_q in pairs:
                if j in SHARED_UNITS:
                    mid = (e0 + e1) // 2
                    nc.scalar.copy(out=dst_v[:, e0:mid], in_=src_q[:, e0:mid])
                    nc.vector.tensor_copy(out=dst_v[:, mid:e1], in_=src_q[:, mid:e1])
                elif j in V_UNITS:
                    nc.vector.tensor_copy(out=dst_v[:, e0:e1], in_=src_q[:, e0:e1])
                else:
                    nc.scalar.copy(out=dst_v[:, e0:e1], in_=src_q[:, e0:e1])

        def regroup_chain(j):
            s, gp, c = units[j]
            engine, e_lo = CHAIN[j]
            iw = 8 if s < 2 else 4
            g_of[j] = ggp.tile([P, (64 - e_lo) * iw, 4], BF16, name="gg", tag="gg", align_bytes=64)
            emit_masks_through(gp, 1024 * s + 1024)
            part = raw[gp][:, :, 1024 * s : 1024 * s + 1024]
            if s < 2:
                src_g = part.rearrange("p t (e o i) -> p o e t i", o=2, i=8)[:, c, e_lo:64]
            else:
                src_g = part.rearrange("p t (e q i) -> p q e t i", q=4, i=4)[:, c, e_lo:64]
            dst_g = g_of[j][:].rearrange("p (e i) t -> p e t i", i=iw)
            if engine == "scalar":
                nc.scalar.copy(out=dst_g, in_=src_g)
            else:
                nc.gpsimd.tensor_scalar(
                    out=dst_g, in0=src_g, scalar1=1.0, scalar2=0.0, op0=mult, op1=add
                )

        def quantise(j):
            s, gp, c = units[j]
            ncol = 512 if s < 2 else 256
            wq = codep.tile([P, ncol], U32, name="wq", tag="wq", align_bytes=64)
            ws = codep.tile([P, ncol], U8, name="ws", tag="ws", align_bytes=64)
            codes[j] = (wq, ws)
            if j not in CHAIN:
                nc.vector.quantize_mx(
                    out=wq[:].bitcast(FP8X4),
                    scales=ws[:],
                    in_=grp_of[j][:].rearrange("p c t -> p (c t)"),
                )
                return
            cut = CHAIN[j][1] * (8 if s < 2 else 4)
            k = CHAIN_ORDER.index(j)
            last = k + 1 == len(CHAIN_ORDER)
            if cut > 0:
                nc.vector.quantize_mx(
                    out=wq[:, 0:cut].bitcast(FP8X4),
                    scales=ws[:, 0:cut],
                    in_=grp_of[j][:].rearrange("p c t -> p (c t)"),
                )
            if last:
                for n in range(WINDOW):
                    emit_exit()
            nc.vector.quantize_mx(
                out=wq[:, cut:ncol].bitcast(FP8X4),
                scales=ws[:, cut:ncol],
                in_=g_of[j][:].rearrange("p c t -> p (c t)"),
            )
            if not last:
                regroup_chain(CHAIN_ORDER[k + 1])
                for n in range(WINDOW):
                    emit_exit()

        def flush_q():
            while st["q"] < len(pend_q):
                j = pend_q[st["q"]]
                st["q"] += 1
                quantise(j)
                pend_mm.append(j)

        def matmuls(j):
            s, gp, c = units[j]
            ncol = 512 if s < 2 else 256
            wq, ws = codes[j]
            for ct in range(4):
                key = (s, c, ct)
                if gp == 0:
                    acc[key] = psum.tile([P, ncol], F32, name="acc", tag="bank")
                    st["open"] += 1
                cs = slice(ct * P, (ct + 1) * P)
                nc.tensor.matmul_mx(
                    out=acc[key][:],
                    lhsT=xq[:, gp, cs].bitcast(FP8X4),
                    lhsT_scale=xs[:, gp, cs],
                    rhs=wq[:].bitcast(FP8X4),
                    rhs_scale=ws[:],
                    start=(gp == 0),
                    stop=(gp == PASSES - 1),
                )
                if gp == PASSES - 1:
                    exit_q.append(key)

        def flush_mm():
            while st["xdone"] and st["mm"] < len(pend_mm):
                j = pend_mm[st["mm"]]
                if units[j][1] == 0 and st["open"] + 4 > 8:
                    return
                st["mm"] += 1
                matmuls(j)

        def emit_exit():
            if st["ex"] >= len(exit_q):
                return
            key = exit_q[st["ex"]]
            st["ex"] += 1
            st["open"] -= 1
            s, c, ct = key
            es = slice(64 * s, 64 * s + 64)
            if s < 2:
                if s == 0:
                    o_sb[(c, ct)] = outp.tile([P, 8, 192], F32, name="o%d_%d" % (c, ct))
                nc.vector.tensor_tensor(
                    out=o_sb[(c, ct)][:, :, es],
                    in0=acc[key][:].rearrange("p (e i) -> p i e", i=8),
                    in1=bias_pe[:, 8 * c : 8 * c + 8, es],
                    op=add,
                )
                if s == 1 and c == 1:
                    nc.sync.dma_start(
                        out=out[ct * P : (ct + 1) * P, 8:16, 0:128],
                        in_=o_sb[(c, ct)][:, :, 0:128],
                    )
            else:
                rows = slice(4 * (c % 2), 4 * (c % 2) + 4)
                ot = o_sb[(c // 2, ct)]
                nc.vector.tensor_tensor(
                    out=ot[:, rows, es],
                    in0=acc[key][:].rearrange("p (e i) -> p i e", i=4),
                    in1=bias_v[:, c, :, es],
                    op=add,
                )
                e_out = slice(0, 192) if c < 2 else es
                nc.sync.dma_start(
                    out=out[ct * P : (ct + 1) * P, 4 * c : 4 * c + 4, e_out],
                    in_=ot[:, rows, e_out],
                )

        def x_quant(item):
            xg, pr, gp = item
            cs = slice(pr * 256, (pr + 1) * 256)
            nc.vector.quantize_mx(
                out=xq[:, gp, cs].bitcast(FP8X4),
                scales=xs[:, gp, cs],
                in_=xg[:].rearrange("p c t -> p (c t)"),
            )

        def x_block():
            flush_q()
            prev = []
            for k in range(8):
                pr, gp = k // 4, k % 4
                xw = x_sb[pr][:].bitcast(F32).rearrange("p c (g w u) -> p c g u w", g=PASSES, u=2)
                xt = psum.tile([P, 2, 256], F32, name="xt", tag="bank")
                for u in range(2):
                    for cl in range(2):
                        nc.tensor.transpose(
                            xt[:, u, cl * P : (cl + 1) * P], xw[:, cl, gp, u, :], ident[:]
                        )
                xg = xgp.tile([P, 256, 4], BF16, name="xg", align_bytes=64)
                nc.scalar.copy(out=xg[:].bitcast(F32), in_=xt[:].rearrange("p u c -> p c u"))
                prev.append((xg, pr, gp))
                if k > 0:
                    x_quant(prev[k - 1])
                emit_masks(X_MASKS)
            x_quant(prev[7])
            st["xdone"] = True
            flush_mm()

        for si in range(2):
            regroup(0, HEAD_E[si])
            regroup(1, HEAD_E[si])
            if si == 0:
                emit_masks_through(0, 1024)
        emit_masks(HEAD_MASKS)
        spread_bias()
        pend_q.append(0)
        pend_q.append(1)
        for j in (2, 3, "X") + tuple(range(4, 32)):
            if j == "X":
                x_block()
            elif j in CHAIN and CHAIN[j][1] == 0:
                pend_q.append(j)
            else:
                regroup(j)
                if j == CHAIN_ORDER[0]:
                    regroup_chain(j)
                if j in V_UNITS:
                    pend_q.append(j)
                else:
                    flush_q()
                    pend_q.append(j)
                    part_a = units[j][0] < 2
                    emit_masks(A_MASKS if part_a else B_MASKS)
                    flush_mm()
                    for n in range(A_EXITS if part_a else B_EXITS):
                        emit_exit()
                    flush_mm()
        flush_q()
        for n in range(64):
            flush_mm()
            emit_exit()
